import numpy as np
import ml_dtypes


def mxq(x, axis, fmt="e4m3"):
    dtype, down = {"e4m3": (ml_dtypes.float8_e4m3fn, 7), "e5m2": (ml_dtypes.float8_e5m2, 14)}[fmt]
    v = np.moveaxis(np.asarray(x, np.float32).astype(ml_dtypes.bfloat16).astype(np.float64), axis, -1)
    blocks = v.reshape(v.shape[:-1] + (-1, 32))
    amax = np.abs(blocks).max(-1, keepdims=True)
    byte = np.maximum(np.where(amax > 0, np.frexp(amax)[1] - 1 + 127, 0) - down, 1)
    scale = np.exp2(byte - 127.0)
    codes = (blocks / scale).astype(np.float32).astype(dtype).astype(np.float64)
    return np.moveaxis((codes * scale).reshape(v.shape), -1, axis)


WIDE = False


def mx_kscale(k):
    if not WIDE:
        return np.ones(k)
    levels = np.array([10, -10, 5, -5, 0])
    if k % 512:
        return np.exp2(np.random.permutation(np.resize(levels, k // 32))).repeat(32)
    a = np.empty((k // 512, 16))
    for p in range(k // 512):
        a[p, :8] = np.random.permutation(np.resize(levels, 8))
        for g in range(8):
            far = levels[np.abs(levels - a[p, g]) >= 10]
            a[p, g + 8] = far[np.random.randint(len(far))]
    return np.exp2(a.ravel()).repeat(32)


BF16 = ml_dtypes.bfloat16


def bf(x):
    return np.asarray(x, np.float32).astype(BF16)


def f64(x):
    return np.asarray(x).astype(np.float64)


B, S, H, N, L = 2, 256, 512, 256, 10
EPS = 1e-06


def setup_inputs():
    s = mx_kscale(H)
    return {"hidden_states": bf(np.random.standard_normal((B, S, H)) * s),
            "conv_w": bf(np.random.standard_normal((L, N, H)) / np.sqrt(H) / s),
            "norm_w": bf(1.0 + 0.1 * np.random.standard_normal(N))}


def reference(hidden_states, conv_w, norm_w):
    x = f64(hidden_states)
    w_sum = f64(conv_w).sum(axis=0)
    out = (mxq(x, 2, "e4m3") @ mxq(w_sum, 1, "e4m3").T) / L
    norm_x = np.sqrt(np.sum(out * out, axis=-1, keepdims=True) + EPS * H)
    x_normed = out / norm_x * np.sqrt(H)
    return x_normed * f64(norm_w)

@@ -1,0 +1,187 @@
+import math
+
+import concourse.mybir as mybir
+from concourse.masks import make_identity
+
+BF16 = mybir.dt.bfloat16
+F32 = mybir.dt.float32
+U32 = mybir.dt.uint32
+U8 = mybir.dt.uint8
+FP8X4 = mybir.dt.float8_e4m3fn_x4
+ADD = mybir.AluOpType.add
+MULT = mybir.AluOpType.mult
+FUNC = mybir.ActivationFunctionType
+
+P = 128
+TOKENS = 512
+H = 512
+CHANNELS = 256
+LAYERS = 10
+EPS = 1e-06
+TOKEN_TILES = TOKENS // P
+CHANNEL_TILES = CHANNELS // P
+HALVES = 2
+PAIR = 2
+PACK = HALVES * PAIR
+
+GPSIMD_COLUMNS = 72
+SPLIT = P - GPSIMD_COLUMNS
+
+X_BEHIND_LAYER = 6
+X_QUANTISED_BEHIND_LAYER = 8
+
+FLOPS = 2 * TOKENS * H * CHANNELS
+
+
+def tile_conv2dlinalgrmsnorm_s_kernel(tc, hidden_states, conv_w, norm_w, out):
+    nc = tc.nc
+    x_dram = hidden_states.flatten_outer_dims().rearrange("(p a) h -> p a h", a=TOKEN_TILES)
+    w_dram = conv_w.rearrange("l (p t) h -> l p t h", t=CHANNEL_TILES)
+    out_dram = out.flatten_outer_dims().rearrange("(p a) c -> p a c", a=TOKEN_TILES)
+
+    with (
+        tc.tile_pool(name="keep", bufs=1) as keep,
+        tc.tile_pool(name="layers", bufs=LAYERS) as layers,
+        tc.tile_pool(name="stage", bufs=4) as stage,
+        tc.psum_pool(name="banks", bufs=8) as banks,
+    ):
+        ident = keep.tile([P, P], F32)
+        make_identity(nc, ident[:])
+        ones = keep.tile([P, P], BF16)
+        nc.vector.memset(ones[:], 1.0)
+        gain_row = keep.tile([P, CHANNELS], BF16)
+        nc.vector.memset(gain_row[:], 0.0)
+        warm = keep.tile([P, 1], F32)
+        nc.vector.memset(warm[:], 1.0)
+        nc.scalar.activation(out=warm[:], in_=warm[:], func=FUNC.Sqrt)
+
+        w_sb = []
+        x_sb = keep.tile([P, TOKEN_TILES, H], BF16)
+        for l in range(LAYERS):
+            w_l = layers.tile([P, CHANNEL_TILES, H], BF16, tag="w")
+            nc.sync.dma_start(out=w_l[:], in_=w_dram[l])
+            w_sb.append(w_l)
+            if l == X_BEHIND_LAYER:
+                nc.sync.dma_start(out=x_sb[:], in_=x_dram)
+                nc.sync.dma_start(out=gain_row[0:1, :], in_=norm_w.unsqueeze(0))
+
+        x_grouped = keep.tile([P, TOKEN_TILES, P, PACK], BF16, align_bytes=64)
+        x_codes = keep.tile([P, TOKENS], U32, align_bytes=64)
+        x_scales = keep.tile([P, TOKENS], U8, align_bytes=64)
+        w_grouped = keep.tile([P, CHANNEL_TILES, P, PACK], BF16, align_bytes=64)
+        w_codes = keep.tile([P, CHANNELS], U32, align_bytes=64)
+        w_scales = keep.tile([P, CHANNELS], U8, align_bytes=64)
+        gain = keep.tile([P, CHANNELS], F32)
+
+        def transpose_x():
+            x_words = x_sb[:].bitcast(F32)
+            x_grouped_words = x_grouped[:].bitcast(F32)
+            for a0 in range(0, TOKEN_TILES, 2):
+                x_t = banks.tile([P, 2, HALVES, P], F32, tag="bank")
+                for a in range(2):
+                    for u in range(HALVES):
+                        nc.tensor.transpose(
+                            x_t[:, a, u, :], x_words[:, a0 + a, u : H // PAIR : HALVES], ident[:]
+                        )
+                nc.scalar.copy(
+                    out=x_grouped_words[:, a0 : a0 + 2],
+                    in_=x_t[:].rearrange("q a u r -> q a r u"),
+                )
+
+        def spread_gain():
+            gain_ps = banks.tile([P, CHANNELS], F32, tag="bank")
+            nc.tensor.matmul(out=gain_ps[:], lhsT=ones[:], rhs=gain_row[:], start=True, stop=True)
+            nc.scalar.activation(
+                out=gain[:], in_=gain_ps[:], func=FUNC.Copy, scale=math.sqrt(H) / LAYERS
+            )
+
+        def add_layer(engine, l, acc, values, grouped):
+            if l < LAYERS - 1:
+                engine.tensor_tensor(out=acc, in0=values, in1=acc, op=ADD)
+            else:
+                engine.tensor_tensor(
+                    out=grouped.rearrange("q p (u e) -> q p u e", e=PAIR),
+                    in0=values.rearrange("q u (p e) -> q p u e", e=PAIR),
+                    in1=acc.rearrange("q u (p e) -> q p u e", e=PAIR),
+                    op=ADD,
+                )
+
+        acc_0 = keep.tile([P, HALVES, P * PAIR], F32)
+        acc_1 = keep.tile([P, HALVES, SPLIT * PAIR], F32)
+        acc_g = keep.tile([P, HALVES, GPSIMD_COLUMNS * PAIR], F32)
+
+        def transposed(l, t):
+            w_t = banks.tile([P, HALVES, P], F32, tag="bank")
+            w_words = w_sb[l][:].bitcast(F32)
+            for u in range(HALVES):
+                nc.tensor.transpose(w_t[:, u, :], w_words[:, t, u : H // PAIR : HALVES], ident[:])
+            return w_t
+
+        for l in range(LAYERS):
+            w_t1 = transposed(l, 1)
+            w_t0 = transposed(l, 0)
+            values_0 = w_t0[:].bitcast(BF16)
+            values_1 = w_t1[:, :, 0:SPLIT].bitcast(BF16)
+            if l == 0:
+                nc.scalar.copy(out=acc_g[:], in_=w_t1[:, :, SPLIT:P].bitcast(BF16))
+                nc.scalar.copy(out=acc_1[:], in_=values_1)
+                nc.vector.tensor_copy(out=acc_0[:], in_=values_0)
+            else:
+                words_g = stage.tile([P, HALVES, GPSIMD_COLUMNS], F32)
+                nc.scalar.copy(out=words_g[:], in_=w_t1[:, :, SPLIT:P])
+                add_layer(nc.gpsimd, l, acc_g[:], words_g[:].bitcast(BF16), w_grouped[:, 1, SPLIT:P])
+                add_layer(nc.vector, l, acc_0[:], values_0, w_grouped[:, 0])
+                add_layer(nc.vector, l, acc_1[:], values_1, w_grouped[:, 1, 0:SPLIT])
+            if l == X_BEHIND_LAYER:
+                transpose_x()
+                spread_gain()
+            if l == X_QUANTISED_BEHIND_LAYER:
+                nc.vector.quantize_mx(
+                    out=x_codes[:].bitcast(FP8X4),
+                    scales=x_scales[:],
+                    in_=x_grouped[:].rearrange("q a r k -> q (a r k)"),
+                )
+
+        nc.vector.quantize_mx(
+            out=w_codes[:].bitcast(FP8X4),
+            scales=w_scales[:],
+            in_=w_grouped[:].rearrange("q t p k -> q (t p k)"),
+        )
+
+        squares = keep.tile([P, CHANNELS], F32)
+        sum_sq = keep.tile([P, TOKEN_TILES], F32)
+        norm = keep.tile([P, TOKEN_TILES], F32)
+        inv_norm = keep.tile([P, TOKEN_TILES], F32)
+        out_sb = keep.tile([P, TOKEN_TILES, CHANNELS], F32)
+        for a in range(TOKEN_TILES):
+            rows = slice(a * P, (a + 1) * P)
+            y = banks.tile([P, CHANNELS], F32, tag="bank")
+            nc.tensor.matmul_mx(
+                out=y[:],
+                lhsT=x_codes[:, rows].bitcast(FP8X4),
+                lhsT_scale=x_scales[:, rows],
+                rhs=w_codes[:].bitcast(FP8X4),
+                rhs_scale=w_scales[:],
+                start=True,
+                stop=True,
+            )
+            nc.scalar.activation(
+                out=squares[:],
+                in_=y[:],
+                func=FUNC.Square,
+                scale=1.0 / LAYERS,
+                accum_out=sum_sq[:, a : a + 1],
+            )
+            nc.scalar.activation(
+                out=norm[:, a : a + 1], in_=sum_sq[:, a : a + 1], func=FUNC.Sqrt, bias=EPS * H
+            )
+            nc.vector.reciprocal(out=inv_norm[:, a : a + 1], in_=norm[:, a : a + 1])
+            nc.vector.scalar_tensor_tensor(
+                out=out_sb[:, a, :].rearrange("r (p t) -> r p t", t=CHANNEL_TILES),
+                in0=y[:].rearrange("r (t p) -> r p t", t=CHANNEL_TILES),
+                scalar=inv_norm[:, a : a + 1],
+                in1=gain[:].rearrange("r (p t) -> r p t", t=CHANNEL_TILES),
+                op0=MULT,
+                op1=MULT,
+            )
+            nc.sync.dma_start(out=out_dram[:, a, :], in_=out_sb[:, a, :])

@@ -20,15 +20,11 @@ LAYERS = 10
 EPS = 1e-06
 TOKEN_TILES = TOKENS // P
 CHANNEL_TILES = CHANNELS // P
-HALVES = 2
+PACK = 4
 PAIR = 2
-PACK = HALVES * PAIR
+HALVES = PACK // PAIR
 
-GPSIMD_COLUMNS = 72
-SPLIT = P - GPSIMD_COLUMNS
-
-X_BEHIND_LAYER = 6
-X_QUANTISED_BEHIND_LAYER = 8
+LAST = LAYERS - 2
 
 FLOPS = 2 * TOKENS * H * CHANNELS
 
@@ -36,14 +32,15 @@ FLOPS = 2 * TOKENS * H * CHANNELS
 def tile_conv2dlinalgrmsnorm_s_kernel(tc, hidden_states, conv_w, norm_w, out):
     nc = tc.nc
     x_dram = hidden_states.flatten_outer_dims().rearrange("(p a) h -> p a h", a=TOKEN_TILES)
-    w_dram = conv_w.rearrange("l (p t) h -> l p t h", t=CHANNEL_TILES)
+    w_dram = conv_w.rearrange("l (p c) h -> p l (c h)", c=CHANNEL_TILES)
+    last_dram = conv_w[LAST:LAYERS].rearrange("l (p c) h -> p l c h", c=CHANNEL_TILES)
     out_dram = out.flatten_outer_dims().rearrange("(p a) c -> p a c", a=TOKEN_TILES)
 
     with (
         tc.tile_pool(name="keep", bufs=1) as keep,
-        tc.tile_pool(name="layers", bufs=LAYERS) as layers,
-        tc.tile_pool(name="stage", bufs=4) as stage,
-        tc.psum_pool(name="banks", bufs=8) as banks,
+        tc.tile_pool(name="terms", bufs=16) as terms,
+        tc.psum_pool(name="sums", bufs=CHANNEL_TILES) as sums,
+        tc.psum_pool(name="banks", bufs=6) as banks,
     ):
         ident = keep.tile([P, P], F32)
         make_identity(nc, ident[:])
@@ -55,15 +52,16 @@ def tile_conv2dlinalgrmsnorm_s_kernel(tc, hidden_states, conv_w, norm_w, out):
         nc.vector.memset(warm[:], 1.0)
         nc.scalar.activation(out=warm[:], in_=warm[:], func=FUNC.Sqrt)
 
-        w_sb = []
         x_sb = keep.tile([P, TOKEN_TILES, H], BF16)
-        for l in range(LAYERS):
-            w_l = layers.tile([P, CHANNEL_TILES, H], BF16, tag="w")
-            nc.sync.dma_start(out=w_l[:], in_=w_dram[l])
-            w_sb.append(w_l)
-            if l == X_BEHIND_LAYER:
-                nc.sync.dma_start(out=x_sb[:], in_=x_dram)
+        nc.sync.dma_start(out=x_sb[:], in_=x_dram)
+        w_sb = keep.tile([P, LAST, CHANNEL_TILES, H], BF16)
+        for l0, l1 in ((0, 1), (1, 3), (3, 5), (5, 7), (7, 8)):
+            nc.sync.dma_start(out=w_sb[:, l0:l1].rearrange("p l c h -> p l (c h)"), in_=w_dram[:, l0:l1])
+            if l0 == 3:
                 nc.sync.dma_start(out=gain_row[0:1, :], in_=norm_w.unsqueeze(0))
+        last_sb = keep.tile([P, CHANNEL_TILES, 2, H], BF16)
+        for c in range(CHANNEL_TILES):
+            nc.sync.dma_start(out=last_sb[:, c], in_=last_dram[:, :, c, :])
 
         x_grouped = keep.tile([P, TOKEN_TILES, P, PACK], BF16, align_bytes=64)
         x_codes = keep.tile([P, TOKENS], U32, align_bytes=64)
@@ -83,7 +81,8 @@ def tile_conv2dlinalgrmsnorm_s_kernel(tc, hidden_states, conv_w, norm_w, out):
                         nc.tensor.transpose(
                             x_t[:, a, u, :], x_words[:, a0 + a, u : H // PAIR : HALVES], ident[:]
                         )
-                nc.scalar.copy(
+                copy = nc.scalar.copy if a0 == 0 else nc.vector.tensor_copy
+                copy(
                     out=x_grouped_words[:, a0 : a0 + 2],
                     in_=x_t[:].rearrange("q a u r -> q a r u"),
                 )
@@ -95,58 +94,68 @@ def tile_conv2dlinalgrmsnorm_s_kernel(tc, hidden_states, conv_w, norm_w, out):
                 out=gain[:], in_=gain_ps[:], func=FUNC.Copy, scale=math.sqrt(H) / LAYERS
             )
 
-        def add_layer(engine, l, acc, values, grouped):
-            if l < LAYERS - 1:
-                engine.tensor_tensor(out=acc, in0=values, in1=acc, op=ADD)
-            else:
-                engine.tensor_tensor(
-                    out=grouped.rearrange("q p (u e) -> q p u e", e=PAIR),
-                    in0=values.rearrange("q u (p e) -> q p u e", e=PAIR),
-                    in1=acc.rearrange("q u (p e) -> q p u e", e=PAIR),
-                    op=ADD,
+        w_sum = []
+        for c in range(CHANNEL_TILES):
+            bank = sums.tile([P, PACK, P], F32, tag="sum")
+            w_sum.append(bank)
+
+        def slots(l, c):
+            rows = w_sb[:, l, c, :] if l < LAST else last_sb[:, c, l - LAST, :]
+            return rows.rearrange("k (q t) -> k t q", t=PACK)
+
+        def accumulate(c, term, ts, first=False, last=False):
+            for t in ts:
+                nc.tensor.matmul(
+                    out=w_sum[c][:, t, :],
+                    lhsT=term[:, t, :],
+                    rhs=ident[:],
+                    start=first and t == 0,
+                    stop=last and t == PACK - 1,
+                    is_transpose=True,
                 )
 
-        acc_0 = keep.tile([P, HALVES, P * PAIR], F32)
-        acc_1 = keep.tile([P, HALVES, SPLIT * PAIR], F32)
-        acc_g = keep.tile([P, HALVES, GPSIMD_COLUMNS * PAIR], F32)
+        def widened(l, c, ts):
+            term = terms.tile([P, PACK, P], F32, tag="term")
+            nc.scalar.copy(out=term[:, ts], in_=slots(l, c)[:, ts])
+            return term
 
-        def transposed(l, t):
-            w_t = banks.tile([P, HALVES, P], F32, tag="bank")
-            w_words = w_sb[l][:].bitcast(F32)
-            for u in range(HALVES):
-                nc.tensor.transpose(w_t[:, u, :], w_words[:, t, u : H // PAIR : HALVES], ident[:])
-            return w_t
+        def pair_sum(l, c, ts):
+            term = terms.tile([P, PACK, P], F32, tag="term")
+            nc.vector.tensor_tensor(
+                out=term[:, ts], in0=slots(l, c)[:, ts], in1=slots(l + 1, c)[:, ts], op=ADD
+            )
+            return term
 
-        for l in range(LAYERS):
-            w_t1 = transposed(l, 1)
-            w_t0 = transposed(l, 0)
-            values_0 = w_t0[:].bitcast(BF16)
-            values_1 = w_t1[:, :, 0:SPLIT].bitcast(BF16)
-            if l == 0:
-                nc.scalar.copy(out=acc_g[:], in_=w_t1[:, :, SPLIT:P].bitcast(BF16))
-                nc.scalar.copy(out=acc_1[:], in_=values_1)
-                nc.vector.tensor_copy(out=acc_0[:], in_=values_0)
-            else:
-                words_g = stage.tile([P, HALVES, GPSIMD_COLUMNS], F32)
-                nc.scalar.copy(out=words_g[:], in_=w_t1[:, :, SPLIT:P])
-                add_layer(nc.gpsimd, l, acc_g[:], words_g[:].bitcast(BF16), w_grouped[:, 1, SPLIT:P])
-                add_layer(nc.vector, l, acc_0[:], values_0, w_grouped[:, 0])
-                add_layer(nc.vector, l, acc_1[:], values_1, w_grouped[:, 1, 0:SPLIT])
-            if l == X_BEHIND_LAYER:
-                transpose_x()
-                spread_gain()
-            if l == X_QUANTISED_BEHIND_LAYER:
-                nc.vector.quantize_mx(
-                    out=x_codes[:].bitcast(FP8X4),
-                    scales=x_scales[:],
-                    in_=x_grouped[:].rearrange("q a r k -> q (a r k)"),
-                )
-
+        every = slice(0, PACK)
+        all_slots = range(PACK)
+        transpose_x()
+        for c in range(CHANNEL_TILES):
+            accumulate(c, widened(0, c, every), all_slots, first=True)
         nc.vector.quantize_mx(
-            out=w_codes[:].bitcast(FP8X4),
-            scales=w_scales[:],
-            in_=w_grouped[:].rearrange("q t p k -> q (t p k)"),
+            out=x_codes[:].bitcast(FP8X4),
+            scales=x_scales[:],
+            in_=x_grouped[:].rearrange("q a r k -> q (a r k)"),
         )
+        for l in (1, 3, 5):
+            for c in range(CHANNEL_TILES):
+                accumulate(c, pair_sum(l, c, every), all_slots)
+        spread_gain()
+        for c in range(CHANNEL_TILES):
+            accumulate(c, widened(7, c, every), all_slots)
+        accumulate(0, pair_sum(LAST, 0, every), all_slots, last=True)
+        for l in (LAST, LAST + 1):
+            accumulate(1, widened(l, 1, slice(0, 1)), range(0, 1))
+        accumulate(1, pair_sum(LAST, 1, slice(1, PACK)), range(1, PACK), last=True)
+
+        nc.scalar.copy(out=w_grouped[:, 0], in_=w_sum[0][:].rearrange("q t k -> q k t"))
+        nc.vector.tensor_copy(out=w_grouped[:, 1], in_=w_sum[1][:].rearrange("q t k -> q k t"))
+        for c in range(CHANNEL_TILES):
+            columns = slice(c * P, (c + 1) * P)
+            nc.vector.quantize_mx(
+                out=w_codes[:, columns].bitcast(FP8X4),
+                scales=w_scales[:, columns],
+                in_=w_grouped[:, c].rearrange("q p k -> q (p k)"),
+            )
 
         squares = keep.tile([P, CHANNELS], F32)
         sum_sq = keep.tile([P, TOKEN_TILES], F32)
@@ -177,10 +186,10 @@ def tile_conv2dlinalgrmsnorm_s_kernel(tc, hidden_states, conv_w, norm_w, out):
             )
             nc.vector.reciprocal(out=inv_norm[:, a : a + 1], in_=norm[:, a : a + 1])
             nc.vector.scalar_tensor_tensor(
-                out=out_sb[:, a, :].rearrange("r (p t) -> r p t", t=CHANNEL_TILES),
-                in0=y[:].rearrange("r (t p) -> r p t", t=CHANNEL_TILES),
+                out=out_sb[:, a, :].rearrange("r (p c) -> r p c", c=CHANNEL_TILES),
+                in0=y[:].rearrange("r (c p) -> r p c", c=CHANNEL_TILES),
                 scalar=inv_norm[:, a : a + 1],
-                in1=gain[:].rearrange("r (p t) -> r p t", t=CHANNEL_TILES),
+                in1=gain[:].rearrange("r (p c) -> r p c", c=CHANNEL_TILES),
                 op0=MULT,
                 op1=MULT,
             )

@@ -53,7 +53,8 @@ def tile_conv2dlinalgrmsnorm_s_kernel(tc, hidden_states, conv_w, norm_w, out):
         nc.scalar.activation(out=warm[:], in_=warm[:], func=FUNC.Sqrt)
 
         x_sb = keep.tile([P, TOKEN_TILES, H], BF16)
-        nc.sync.dma_start(out=x_sb[:], in_=x_dram)
+        for a0 in range(0, TOKEN_TILES, 2):
+            nc.sync.dma_start(out=x_sb[:, a0 : a0 + 2], in_=x_dram[:, a0 : a0 + 2])
         w_sb = keep.tile([P, LAST, CHANNEL_TILES, H], BF16)
         for l0, l1 in ((0, 1), (1, 3), (3, 5), (5, 7), (7, 8)):
             nc.sync.dma_start(out=w_sb[:, l0:l1].rearrange("p l c h -> p l (c h)"), in_=w_dram[:, l0:l1])
@@ -72,16 +73,16 @@ def tile_conv2dlinalgrmsnorm_s_kernel(tc, hidden_states, conv_w, norm_w, out):
         gain = keep.tile([P, CHANNELS], F32)
 
         def transpose_x():
-            x_words = x_sb[:].bitcast(F32)
+            x_words = x_sb[:].bitcast(F32).rearrange("r a (q u) -> r a u q", u=HALVES)
             x_grouped_words = x_grouped[:].bitcast(F32)
             for a0 in range(0, TOKEN_TILES, 2):
+                copy = nc.scalar.copy if a0 == 0 else nc.vector.tensor_copy
+                x_apart = keep.tile([P, 2, HALVES, P], F32, name="x_apart%d" % a0)
+                copy(out=x_apart[:], in_=x_words[:, a0 : a0 + 2])
                 x_t = banks.tile([P, 2, HALVES, P], F32, tag="bank")
                 for a in range(2):
                     for u in range(HALVES):
-                        nc.tensor.transpose(
-                            x_t[:, a, u, :], x_words[:, a0 + a, u : H // PAIR : HALVES], ident[:]
-                        )
-                copy = nc.scalar.copy if a0 == 0 else nc.vector.tensor_copy
+                        nc.tensor.transpose(x_t[:, a, u, :], x_apart[:, a, u, :], ident[:])
                 copy(
                     out=x_grouped_words[:, a0 : a0 + 2],
                     in_=x_t[:].rearrange("q a u r -> q a r u"),

@@ -102,7 +102,7 @@ def tile_conv2dlinalgrmsnorm_s_kernel(tc, hidden_states, conv_w, norm_w, out):
 
         def slots(l, c):
             rows = w_sb[:, l, c, :] if l < LAST else last_sb[:, c, l - LAST, :]
-            return rows.rearrange("k (q t) -> k t q", t=PACK)
+            return rows.rearrange("k (q t) -> k q t", t=PACK)
 
         def accumulate(c, term, ts, first=False, last=False):
             for t in ts:
@@ -117,13 +117,18 @@ def tile_conv2dlinalgrmsnorm_s_kernel(tc, hidden_states, conv_w, norm_w, out):
 
         def widened(l, c, ts):
             term = terms.tile([P, PACK, P], F32, tag="term")
-            nc.scalar.copy(out=term[:, ts], in_=slots(l, c)[:, ts])
+            nc.scalar.copy(
+                out=term[:, ts].rearrange("k t q -> k q t"), in_=slots(l, c)[:, :, ts]
+            )
             return term
 
         def pair_sum(l, c, ts):
             term = terms.tile([P, PACK, P], F32, tag="term")
             nc.vector.tensor_tensor(
-                out=term[:, ts], in0=slots(l, c)[:, ts], in1=slots(l + 1, c)[:, ts], op=ADD
+                out=term[:, ts].rearrange("k t q -> k q t"),
+                in0=slots(l, c)[:, :, ts],
+                in1=slots(l + 1, c)[:, :, ts],
+                op=ADD,
             )
             return term
 

@@ -39,8 +39,10 @@ def tile_conv2dlinalgrmsnorm_s_kernel(tc, hidden_states, conv_w, norm_w, out):
     with (
         tc.tile_pool(name="keep", bufs=1) as keep,
         tc.tile_pool(name="terms", bufs=16) as terms,
+        tc.tile_pool(name="stage", bufs=TOKEN_TILES) as stage,
         tc.psum_pool(name="sums", bufs=CHANNEL_TILES) as sums,
         tc.psum_pool(name="banks", bufs=6) as banks,
+        tc.manual_schedule(),
     ):
         ident = keep.tile([P, P], F32)
         make_identity(nc, ident[:])
@@ -50,19 +52,21 @@ def tile_conv2dlinalgrmsnorm_s_kernel(tc, hidden_states, conv_w, norm_w, out):
         nc.vector.memset(gain_row[:], 0.0)
         warm = keep.tile([P, 1], F32)
         nc.vector.memset(warm[:], 1.0)
-        nc.scalar.activation(out=warm[:], in_=warm[:], func=FUNC.Sqrt)
+        nc.scalar.activation(out=warm[:], in_=warm[:], func=FUNC.Abs_reciprocal_sqrt)
 
         x_sb = keep.tile([P, TOKEN_TILES, H], BF16)
-        for a0 in range(0, TOKEN_TILES, 2):
-            nc.sync.dma_start(out=x_sb[:, a0 : a0 + 2], in_=x_dram[:, a0 : a0 + 2])
+        nc.sync.dma_start(out=x_sb[:, 0:2], in_=x_dram[:, 0:2])
         w_sb = keep.tile([P, LAST, CHANNEL_TILES, H], BF16)
-        for l0, l1 in ((0, 1), (1, 3), (3, 5), (5, 7), (7, 8)):
-            nc.sync.dma_start(out=w_sb[:, l0:l1].rearrange("p l c h -> p l (c h)"), in_=w_dram[:, l0:l1])
-            if l0 == 3:
+        for l0, l1 in ((0, 2), (2, 4), (4, 6), (6, 8)):
+            nc.sync.dma_start(
+                out=w_sb[:, l0:l1].rearrange("p l c h -> p l (c h)"), in_=w_dram[:, l0:l1]
+            )
+            if l0 == 0:
                 nc.sync.dma_start(out=gain_row[0:1, :], in_=norm_w.unsqueeze(0))
         last_sb = keep.tile([P, CHANNEL_TILES, 2, H], BF16)
         for c in range(CHANNEL_TILES):
             nc.sync.dma_start(out=last_sb[:, c], in_=last_dram[:, :, c, :])
+        nc.sync.dma_start(out=x_sb[:, 2:4], in_=x_dram[:, 2:4])
 
         x_grouped = keep.tile([P, TOKEN_TILES, P, PACK], BF16, align_bytes=64)
         x_codes = keep.tile([P, TOKENS], U32, align_bytes=64)
@@ -72,21 +76,27 @@ def tile_conv2dlinalgrmsnorm_s_kernel(tc, hidden_states, conv_w, norm_w, out):
         w_scales = keep.tile([P, CHANNELS], U8, align_bytes=64)
         gain = keep.tile([P, CHANNELS], F32)
 
-        def transpose_x():
+        def transpose_x(a0, spread):
             x_words = x_sb[:].bitcast(F32).rearrange("r a (q u) -> r a u q", u=HALVES)
             x_grouped_words = x_grouped[:].bitcast(F32)
-            for a0 in range(0, TOKEN_TILES, 2):
-                copy = nc.scalar.copy if a0 == 0 else nc.vector.tensor_copy
-                x_apart = keep.tile([P, 2, HALVES, P], F32, name="x_apart%d" % a0)
-                copy(out=x_apart[:], in_=x_words[:, a0 : a0 + 2])
-                x_t = banks.tile([P, 2, HALVES, P], F32, tag="bank")
-                for a in range(2):
-                    for u in range(HALVES):
-                        nc.tensor.transpose(x_t[:, a, u, :], x_apart[:, a, u, :], ident[:])
-                copy(
-                    out=x_grouped_words[:, a0 : a0 + 2],
-                    in_=x_t[:].rearrange("q a u r -> q a r u"),
-                )
+            x_apart = keep.tile([P, 2, HALVES, P], F32, name="x_apart%d" % a0)
+            spread(out=x_apart[:], in_=x_words[:, a0 : a0 + 2])
+            x_t = banks.tile([P, 2, HALVES, P], F32, tag="bank")
+            for a in range(2):
+                for u in range(HALVES):
+                    nc.tensor.transpose(x_t[:, a, u, :], x_apart[:, a, u, :], ident[:])
+            return lambda: nc.scalar.copy(
+                out=x_grouped_words[:, a0 : a0 + 2],
+                in_=x_t[:].rearrange("q a u r -> q a r u"),
+            )
+
+        def quantise_x(a0):
+            rows = slice(a0 * P, (a0 + 2) * P)
+            nc.vector.quantize_mx(
+                out=x_codes[:, rows].bitcast(FP8X4),
+                scales=x_scales[:, rows],
+                in_=x_grouped[:, a0 : a0 + 2].rearrange("q a r k -> q (a r k)"),
+            )
 
         def spread_gain():
             gain_ps = banks.tile([P, CHANNELS], F32, tag="bank")
@@ -134,28 +144,7 @@ def tile_conv2dlinalgrmsnorm_s_kernel(tc, hidden_states, conv_w, norm_w, out):
 
         every = slice(0, PACK)
         all_slots = range(PACK)
-        transpose_x()
-        for c in range(CHANNEL_TILES):
-            accumulate(c, widened(0, c, every), all_slots, first=True)
-        nc.vector.quantize_mx(
-            out=x_codes[:].bitcast(FP8X4),
-            scales=x_scales[:],
-            in_=x_grouped[:].rearrange("q a r k -> q (a r k)"),
-        )
-        for l in (1, 3, 5):
-            for c in range(CHANNEL_TILES):
-                accumulate(c, pair_sum(l, c, every), all_slots)
-        spread_gain()
-        for c in range(CHANNEL_TILES):
-            accumulate(c, widened(7, c, every), all_slots)
-        accumulate(0, pair_sum(LAST, 0, every), all_slots, last=True)
-        for l in (LAST, LAST + 1):
-            accumulate(1, widened(l, 1, slice(0, 1)), range(0, 1))
-        accumulate(1, pair_sum(LAST, 1, slice(1, PACK)), range(1, PACK), last=True)
-
-        nc.scalar.copy(out=w_grouped[:, 0], in_=w_sum[0][:].rearrange("q t k -> q k t"))
-        nc.vector.tensor_copy(out=w_grouped[:, 1], in_=w_sum[1][:].rearrange("q t k -> q k t"))
-        for c in range(CHANNEL_TILES):
+        def quantise_w(c):
             columns = slice(c * P, (c + 1) * P)
             nc.vector.quantize_mx(
                 out=w_codes[:, columns].bitcast(FP8X4),
@@ -163,16 +152,37 @@ def tile_conv2dlinalgrmsnorm_s_kernel(tc, hidden_states, conv_w, norm_w, out):
                 in_=w_grouped[:, c].rearrange("q p k -> q (p k)"),
             )
 
-        squares = keep.tile([P, CHANNELS], F32)
+        transpose_x(0, nc.scalar.copy)()
+        for l in (0, 2, 4):
+            for c in range(CHANNEL_TILES):
+                accumulate(c, pair_sum(l, c, every), all_slots, first=l == 0)
+            if l == 0:
+                spread_gain()
+        accumulate(1, widened(6, 1, every), all_slots)
+        accumulate(0, pair_sum(6, 0, every), all_slots)
+        accumulate(1, widened(7, 1, every), all_slots)
+        accumulate(0, pair_sum(LAST, 0, every), all_slots, last=True)
+        for l in (LAST, LAST + 1):
+            accumulate(1, widened(l, 1, slice(0, 1)), range(0, 1))
+        accumulate(1, pair_sum(LAST, 1, slice(1, PACK)), range(1, PACK), last=True)
+        copy_x2 = transpose_x(2, nc.vector.tensor_copy)
+        quantise_x(0)
+        nc.scalar.copy(out=w_grouped[:, 0], in_=w_sum[0][:].rearrange("q t k -> q k t"))
+        nc.vector.tensor_copy(out=w_grouped[:, 1], in_=w_sum[1][:].rearrange("q t k -> q k t"))
+        quantise_w(0)
+        quantise_w(1)
+        copy_x2()
+        quantise_x(2)
+
         sum_sq = keep.tile([P, TOKEN_TILES], F32)
-        norm = keep.tile([P, TOKEN_TILES], F32)
         inv_norm = keep.tile([P, TOKEN_TILES], F32)
         out_sb = keep.tile([P, TOKEN_TILES, CHANNELS], F32)
+        y = []
         for a in range(TOKEN_TILES):
             rows = slice(a * P, (a + 1) * P)
-            y = banks.tile([P, CHANNELS], F32, tag="bank")
+            y_a = banks.tile([P, CHANNELS], F32, tag="bank")
             nc.tensor.matmul_mx(
-                out=y[:],
+                out=y_a[:],
                 lhsT=x_codes[:, rows].bitcast(FP8X4),
                 lhsT_scale=x_scales[:, rows],
                 rhs=w_codes[:].bitcast(FP8X4),
@@ -180,23 +190,37 @@ def tile_conv2dlinalgrmsnorm_s_kernel(tc, hidden_states, conv_w, norm_w, out):
                 start=True,
                 stop=True,
             )
+            y.append(y_a)
+
+        def square(a):
+            squares = stage.tile([P, CHANNELS], F32)
             nc.scalar.activation(
                 out=squares[:],
-                in_=y[:],
+                in_=y[a][:],
                 func=FUNC.Square,
                 scale=1.0 / LAYERS,
                 accum_out=sum_sq[:, a : a + 1],
             )
+
+        def normalise(a):
             nc.scalar.activation(
-                out=norm[:, a : a + 1], in_=sum_sq[:, a : a + 1], func=FUNC.Sqrt, bias=EPS * H
+                out=inv_norm[:, a : a + 1],
+                in_=sum_sq[:, a : a + 1],
+                func=FUNC.Abs_reciprocal_sqrt,
+                bias=EPS * H,
             )
-            nc.vector.reciprocal(out=inv_norm[:, a : a + 1], in_=norm[:, a : a + 1])
             nc.vector.scalar_tensor_tensor(
                 out=out_sb[:, a, :].rearrange("r (p c) -> r p c", c=CHANNEL_TILES),
-                in0=y[:].rearrange("r (c p) -> r p c", c=CHANNEL_TILES),
+                in0=y[a][:].rearrange("r (c p) -> r p c", c=CHANNEL_TILES),
                 scalar=inv_norm[:, a : a + 1],
                 in1=gain[:].rearrange("r (p c) -> r p c", c=CHANNEL_TILES),
                 op0=MULT,
                 op1=MULT,
             )
             nc.sync.dma_start(out=out_dram[:, a, :], in_=out_sb[:, a, :])
+
+        square(0)
+        for a in range(TOKEN_TILES):
+            if a + 1 < TOKEN_TILES:
+                square(a + 1)
+            normalise(a)

@@ -112,7 +112,7 @@ def tile_conv2dlinalgrmsnorm_s_kernel(tc, hidden_states, conv_w, norm_w, out):
 
         def slots(l, c):
             rows = w_sb[:, l, c, :] if l < LAST else last_sb[:, c, l - LAST, :]
-            return rows.rearrange("k (q t) -> k q t", t=PACK)
+            return rows.rearrange("k (g q t) -> k g t q", q=2, t=PACK)
 
         def accumulate(c, term, ts, first=False, last=False):
             for t in ts:
@@ -128,14 +128,14 @@ def tile_conv2dlinalgrmsnorm_s_kernel(tc, hidden_states, conv_w, norm_w, out):
         def widened(l, c, ts):
             term = terms.tile([P, PACK, P], F32, tag="term")
             nc.scalar.copy(
-                out=term[:, ts].rearrange("k t q -> k q t"), in_=slots(l, c)[:, :, ts]
+                out=term[:, ts].rearrange("k t (g q) -> k g t q", q=2), in_=slots(l, c)[:, :, ts]
             )
             return term
 
         def pair_sum(l, c, ts):
             term = terms.tile([P, PACK, P], F32, tag="term")
             nc.vector.tensor_tensor(
-                out=term[:, ts].rearrange("k t q -> k q t"),
+                out=term[:, ts].rearrange("k t (g q) -> k g t q", q=2),
                 in0=slots(l, c)[:, :, ts],
                 in1=slots(l + 1, c)[:, :, ts],
                 op=ADD,

@@ -46,10 +46,10 @@ def tile_conv2dlinalgrmsnorm_s_kernel(tc, hidden_states, conv_w, norm_w, out):
     ):
         ident = keep.tile([P, P], F32)
         make_identity(nc, ident[:])
-        ones = keep.tile([P, P], BF16)
-        nc.vector.memset(ones[:], 1.0)
-        gain_row = keep.tile([P, CHANNELS], BF16)
-        nc.vector.memset(gain_row[:], 0.0)
+        ident_bf16 = keep.tile([P, P], BF16)
+        nc.vector.tensor_copy(out=ident_bf16[:], in_=ident[:])
+        gain_rows = keep.tile([P, P], BF16)
+        nc.vector.memset(gain_rows[:], 0.0)
         warm = keep.tile([P, 1], F32)
         nc.vector.memset(warm[:], 1.0)
         nc.scalar.activation(out=warm[:], in_=warm[:], func=FUNC.Abs_reciprocal_sqrt)
@@ -62,7 +62,9 @@ def tile_conv2dlinalgrmsnorm_s_kernel(tc, hidden_states, conv_w, norm_w, out):
                 out=w_sb[:, l0:l1].rearrange("p l c h -> p l (c h)"), in_=w_dram[:, l0:l1]
             )
             if l0 == 0:
-                nc.sync.dma_start(out=gain_row[0:1, :], in_=norm_w.unsqueeze(0))
+                nc.sync.dma_start(
+                    out=gain_rows[0:2, :], in_=norm_w.rearrange("(r n) -> r n", r=2)
+                )
         last_sb = keep.tile([P, CHANNEL_TILES, 2, H], BF16)
         for c in range(CHANNEL_TILES):
             nc.sync.dma_start(out=last_sb[:, c], in_=last_dram[:, :, c, :])
@@ -98,9 +100,21 @@ def tile_conv2dlinalgrmsnorm_s_kernel(tc, hidden_states, conv_w, norm_w, out):
                 in_=x_grouped[:, a0 : a0 + 2].rearrange("q a r k -> q (a r k)"),
             )
 
-        def spread_gain():
-            gain_ps = banks.tile([P, CHANNELS], F32, tag="bank")
-            nc.tensor.matmul(out=gain_ps[:], lhsT=ones[:], rhs=gain_row[:], start=True, stop=True)
+        def turn_gain():
+            columns_ps = banks.tile([P, P], BF16, tag="bank")
+            nc.tensor.transpose(columns_ps[:], gain_rows[:], ident_bf16[:])
+            columns = keep.tile([P, 2], BF16)
+            nc.scalar.copy(out=columns[:], in_=columns_ps[:, 0:2])
+            return columns
+
+        def spread_gain(columns):
+            gain_ps = banks.tile([P, CHANNELS], BF16, tag="bank")
+            for r in range(2):
+                nc.tensor.transpose(
+                    gain_ps[:, r * P : (r + 1) * P],
+                    columns[:, r : r + 1].to_broadcast([P, P]),
+                    ident_bf16[:],
+                )
             nc.scalar.activation(
                 out=gain[:], in_=gain_ps[:], func=FUNC.Copy, scale=math.sqrt(H) / LAYERS
             )
@@ -114,7 +128,7 @@ def tile_conv2dlinalgrmsnorm_s_kernel(tc, hidden_states, conv_w, norm_w, out):
             rows = w_sb[:, l, c, :] if l < LAST else last_sb[:, c, l - LAST, :]
             return rows.rearrange("k (g q t) -> k g t q", q=2, t=PACK)
 
-        def accumulate(c, term, ts, first=False, last=False):
+        def accumulate(c, term, ts, first=False, last=False, plain=()):
             for t in ts:
                 nc.tensor.matmul(
                     out=w_sum[c][:, t, :],
@@ -122,7 +136,7 @@ def tile_conv2dlinalgrmsnorm_s_kernel(tc, hidden_states, conv_w, norm_w, out):
                     rhs=ident[:],
                     start=first and t == 0,
                     stop=last and t == PACK - 1,
-                    is_transpose=True,
+                    is_transpose=t not in plain,
                 )
 
         def widened(l, c, ts):
@@ -155,13 +169,14 @@ def tile_conv2dlinalgrmsnorm_s_kernel(tc, hidden_states, conv_w, norm_w, out):
         transpose_x(0, nc.scalar.copy)()
         for l in (0, 2, 4):
             for c in range(CHANNEL_TILES):
-                accumulate(c, pair_sum(l, c, every), all_slots, first=l == 0)
+                plain = (3,) if (l, c) in ((0, 1), (4, 0)) else ()
+                accumulate(c, pair_sum(l, c, every), all_slots, first=l == 0, plain=plain)
             if l == 0:
-                spread_gain()
+                gain_columns = turn_gain()
         accumulate(1, widened(6, 1, every), all_slots)
         accumulate(0, pair_sum(6, 0, every), all_slots)
         accumulate(1, widened(7, 1, every), all_slots)
-        accumulate(0, pair_sum(LAST, 0, every), all_slots, last=True)
+        accumulate(0, pair_sum(LAST, 0, every), all_slots, last=True, plain=(3,))
         for l in (LAST, LAST + 1):
             accumulate(1, widened(l, 1, slice(0, 1)), range(0, 1))
         accumulate(1, pair_sum(LAST, 1, slice(1, PACK)), range(1, PACK), last=True)
@@ -172,6 +187,7 @@ def tile_conv2dlinalgrmsnorm_s_kernel(tc, hidden_states, conv_w, norm_w, out):
         quantise_w(0)
         quantise_w(1)
         copy_x2()
+        spread_gain(gain_columns)
         quantise_x(2)
 
         sum_sq = keep.tile([P, TOKEN_TILES], F32)

@@ -1,5 +1,3 @@
-import math
-
 import concourse.mybir as mybir
 from concourse.masks import make_identity
 
@@ -46,25 +44,25 @@ def tile_conv2dlinalgrmsnorm_s_kernel(tc, hidden_states, conv_w, norm_w, out):
     ):
         ident = keep.tile([P, P], F32)
         make_identity(nc, ident[:])
-        ident_bf16 = keep.tile([P, P], BF16)
-        nc.vector.tensor_copy(out=ident_bf16[:], in_=ident[:])
         gain_rows = keep.tile([P, P], BF16)
         nc.vector.memset(gain_rows[:], 0.0)
+        ident_bf16 = keep.tile([P, P], BF16)
+        nc.vector.tensor_copy(out=ident_bf16[:], in_=ident[:])
         warm = keep.tile([P, 1], F32)
         nc.vector.memset(warm[:], 1.0)
         nc.scalar.activation(out=warm[:], in_=warm[:], func=FUNC.Abs_reciprocal_sqrt)
 
-        x_sb = keep.tile([P, TOKEN_TILES, H], BF16)
-        nc.sync.dma_start(out=x_sb[:, 0:2], in_=x_dram[:, 0:2])
         w_sb = keep.tile([P, LAST, CHANNEL_TILES, H], BF16)
-        for l0, l1 in ((0, 2), (2, 4), (4, 6), (6, 8)):
+        for l in range(0, LAST, 2):
             nc.sync.dma_start(
-                out=w_sb[:, l0:l1].rearrange("p l c h -> p l (c h)"), in_=w_dram[:, l0:l1]
+                out=w_sb[:, l : l + 2].rearrange("p l c h -> p l (c h)"), in_=w_dram[:, l : l + 2]
             )
-            if l0 == 0:
+            if l == 0:
                 nc.sync.dma_start(
                     out=gain_rows[0:2, :], in_=norm_w.rearrange("(r n) -> r n", r=2)
                 )
+        x_sb = keep.tile([P, TOKEN_TILES, H], BF16)
+        nc.sync.dma_start(out=x_sb[:, 0:2], in_=x_dram[:, 0:2])
         last_sb = keep.tile([P, CHANNEL_TILES, 2, H], BF16)
         for c in range(CHANNEL_TILES):
             nc.sync.dma_start(out=last_sb[:, c], in_=last_dram[:, :, c, :])
@@ -76,7 +74,7 @@ def tile_conv2dlinalgrmsnorm_s_kernel(tc, hidden_states, conv_w, norm_w, out):
         w_grouped = keep.tile([P, CHANNEL_TILES, P, PACK], BF16, align_bytes=64)
         w_codes = keep.tile([P, CHANNELS], U32, align_bytes=64)
         w_scales = keep.tile([P, CHANNELS], U8, align_bytes=64)
-        gain = keep.tile([P, CHANNELS], F32)
+        gain = keep.tile([P, CHANNELS], BF16)
 
         def transpose_x(a0, spread):
             x_words = x_sb[:].bitcast(F32).rearrange("r a (q u) -> r a u q", u=HALVES)
@@ -115,9 +113,7 @@ def tile_conv2dlinalgrmsnorm_s_kernel(tc, hidden_states, conv_w, norm_w, out):
                     columns[:, r : r + 1].to_broadcast([P, P]),
                     ident_bf16[:],
                 )
-            nc.scalar.activation(
-                out=gain[:], in_=gain_ps[:], func=FUNC.Copy, scale=math.sqrt(H) / LAYERS
-            )
+            nc.scalar.copy(out=gain[:], in_=gain_ps[:])
 
         w_sum = []
         for c in range(CHANNEL_TILES):
@@ -158,36 +154,33 @@ def tile_conv2dlinalgrmsnorm_s_kernel(tc, hidden_states, conv_w, norm_w, out):
 
         every = slice(0, PACK)
         all_slots = range(PACK)
-        def quantise_w(c):
-            columns = slice(c * P, (c + 1) * P)
+        def quantise_w():
             nc.vector.quantize_mx(
-                out=w_codes[:, columns].bitcast(FP8X4),
-                scales=w_scales[:, columns],
-                in_=w_grouped[:, c].rearrange("q p k -> q (p k)"),
+                out=w_codes[:].bitcast(FP8X4),
+                scales=w_scales[:],
+                in_=w_grouped[:].rearrange("q c p k -> q (c p k)"),
             )
 
-        transpose_x(0, nc.scalar.copy)()
-        for l in (0, 2, 4):
+        for l in range(0, LAST, 2):
             for c in range(CHANNEL_TILES):
-                plain = (3,) if (l, c) in ((0, 1), (4, 0)) else ()
+                plain = (3,) if (l, c) in ((0, 1), (4, 0), (6, 1)) else ()
                 accumulate(c, pair_sum(l, c, every), all_slots, first=l == 0, plain=plain)
-            if l == 0:
-                gain_columns = turn_gain()
-        accumulate(1, widened(6, 1, every), all_slots)
-        accumulate(0, pair_sum(6, 0, every), all_slots)
-        accumulate(1, widened(7, 1, every), all_slots)
-        accumulate(0, pair_sum(LAST, 0, every), all_slots, last=True, plain=(3,))
+                if (l, c) == (0, 1):
+                    gain_columns = turn_gain()
+                if (l, c) == (2, 1):
+                    spread_gain(gain_columns)
+        copy_x0 = transpose_x(0, nc.scalar.copy)
+        accumulate(0, pair_sum(LAST, 0, every), all_slots, last=True)
         for l in (LAST, LAST + 1):
             accumulate(1, widened(l, 1, slice(0, 1)), range(0, 1))
         accumulate(1, pair_sum(LAST, 1, slice(1, PACK)), range(1, PACK), last=True)
+        copy_x0()
         copy_x2 = transpose_x(2, nc.vector.tensor_copy)
-        quantise_x(0)
         nc.scalar.copy(out=w_grouped[:, 0], in_=w_sum[0][:].rearrange("q t k -> q k t"))
         nc.vector.tensor_copy(out=w_grouped[:, 1], in_=w_sum[1][:].rearrange("q t k -> q k t"))
-        quantise_w(0)
-        quantise_w(1)
+        quantise_x(0)
+        quantise_w()
         copy_x2()
-        spread_gain(gain_columns)
         quantise_x(2)
 
         sum_sq = keep.tile([P, TOKEN_TILES], F32)
@@ -214,7 +207,6 @@ def tile_conv2dlinalgrmsnorm_s_kernel(tc, hidden_states, conv_w, norm_w, out):
                 out=squares[:],
                 in_=y[a][:],
                 func=FUNC.Square,
-                scale=1.0 / LAYERS,
                 accum_out=sum_sq[:, a : a + 1],
             )
 
@@ -223,7 +215,8 @@ def tile_conv2dlinalgrmsnorm_s_kernel(tc, hidden_states, conv_w, norm_w, out):
                 out=inv_norm[:, a : a + 1],
                 in_=sum_sq[:, a : a + 1],
                 func=FUNC.Abs_reciprocal_sqrt,
-                bias=EPS * H,
+                scale=1.0 / H,
+                bias=EPS * LAYERS**2,
             )
             nc.vector.scalar_tensor_tensor(
                 out=out_sb[:, a, :].rearrange("r (p c) -> r p c", c=CHANNEL_TILES),

@@ -154,11 +154,12 @@ def tile_conv2dlinalgrmsnorm_s_kernel(tc, hidden_states, conv_w, norm_w, out):
 
         every = slice(0, PACK)
         all_slots = range(PACK)
-        def quantise_w():
+        def quantise_w(c):
+            columns = slice(c * P, (c + 1) * P)
             nc.vector.quantize_mx(
-                out=w_codes[:].bitcast(FP8X4),
-                scales=w_scales[:],
-                in_=w_grouped[:].rearrange("q c p k -> q (c p k)"),
+                out=w_codes[:, columns].bitcast(FP8X4),
+                scales=w_scales[:, columns],
+                in_=w_grouped[:, c].rearrange("q p k -> q (p k)"),
             )
 
         for l in range(0, LAST, 2):
@@ -176,10 +177,11 @@ def tile_conv2dlinalgrmsnorm_s_kernel(tc, hidden_states, conv_w, norm_w, out):
         accumulate(1, pair_sum(LAST, 1, slice(1, PACK)), range(1, PACK), last=True)
         copy_x0()
         copy_x2 = transpose_x(2, nc.vector.tensor_copy)
-        nc.scalar.copy(out=w_grouped[:, 0], in_=w_sum[0][:].rearrange("q t k -> q k t"))
-        nc.vector.tensor_copy(out=w_grouped[:, 1], in_=w_sum[1][:].rearrange("q t k -> q k t"))
+        nc.vector.tensor_copy(out=w_grouped[:, 0], in_=w_sum[0][:].rearrange("q t k -> q k t"))
+        nc.scalar.copy(out=w_grouped[:, 1], in_=w_sum[1][:].rearrange("q t k -> q k t"))
         quantise_x(0)
-        quantise_w()
+        quantise_w(0)
+        quantise_w(1)
         copy_x2()
         quantise_x(2)
 

import concourse.mybir as mybir
from concourse.masks import make_identity

BF16 = mybir.dt.bfloat16
F32 = mybir.dt.float32
U32 = mybir.dt.uint32
U8 = mybir.dt.uint8
FP8X4 = mybir.dt.float8_e4m3fn_x4
ADD = mybir.AluOpType.add
MULT = mybir.AluOpType.mult
FUNC = mybir.ActivationFunctionType

P = 128
TOKENS = 512
H = 512
CHANNELS = 256
LAYERS = 10
EPS = 1e-06
TOKEN_TILES = TOKENS // P
CHANNEL_TILES = CHANNELS // P
PACK = 4
PAIR = 2
HALVES = PACK // PAIR

LAST = LAYERS - 2

FLOPS = 2 * TOKENS * H * CHANNELS


def tile_conv2dlinalgrmsnorm_s_kernel(tc, hidden_states, conv_w, norm_w, out):
    nc = tc.nc
    x_dram = hidden_states.flatten_outer_dims().rearrange("(p a) h -> p a h", a=TOKEN_TILES)
    w_dram = conv_w.rearrange("l (p c) h -> p l (c h)", c=CHANNEL_TILES)
    last_dram = conv_w[LAST:LAYERS].rearrange("l (p c) h -> p l c h", c=CHANNEL_TILES)
    out_dram = out.flatten_outer_dims().rearrange("(p a) c -> p a c", a=TOKEN_TILES)

    with (
        tc.tile_pool(name="keep", bufs=1) as keep,
        tc.tile_pool(name="terms", bufs=16) as terms,
        tc.tile_pool(name="stage", bufs=TOKEN_TILES) as stage,
        tc.psum_pool(name="sums", bufs=CHANNEL_TILES) as sums,
        tc.psum_pool(name="banks", bufs=6) as banks,
        tc.manual_schedule(),
    ):
        ident = keep.tile([P, P], F32)
        make_identity(nc, ident[:])
        gain_rows = keep.tile([P, P], BF16)
        nc.vector.memset(gain_rows[:], 0.0)
        ident_bf16 = keep.tile([P, P], BF16)
        nc.vector.tensor_copy(out=ident_bf16[:], in_=ident[:])
        warm = keep.tile([P, 1], F32)
        nc.vector.memset(warm[:], 1.0)
        nc.scalar.activation(out=warm[:], in_=warm[:], func=FUNC.Abs_reciprocal_sqrt)

        w_sb = keep.tile([P, LAST, CHANNEL_TILES, H], BF16)
        for l in range(0, LAST, 2):
            nc.sync.dma_start(
                out=w_sb[:, l : l + 2].rearrange("p l c h -> p l (c h)"), in_=w_dram[:, l : l + 2]
            )
            if l == 0:
                nc.sync.dma_start(
                    out=gain_rows[0:2, :], in_=norm_w.rearrange("(r n) -> r n", r=2)
                )
        x_sb = keep.tile([P, TOKEN_TILES, H], BF16)
        nc.sync.dma_start(out=x_sb[:, 0:2], in_=x_dram[:, 0:2])
        last_sb = keep.tile([P, CHANNEL_TILES, 2, H], BF16)
        for c in range(CHANNEL_TILES):
            nc.sync.dma_start(out=last_sb[:, c], in_=last_dram[:, :, c, :])
        nc.sync.dma_start(out=x_sb[:, 2:4], in_=x_dram[:, 2:4])

        x_grouped = keep.tile([P, TOKEN_TILES, P, PACK], BF16, align_bytes=64)
        x_codes = keep.tile([P, TOKENS], U32, align_bytes=64)
        x_scales = keep.tile([P, TOKENS], U8, align_bytes=64)
        w_grouped = keep.tile([P, CHANNEL_TILES, P, PACK], BF16, align_bytes=64)
        w_codes = keep.tile([P, CHANNELS], U32, align_bytes=64)
        w_scales = keep.tile([P, CHANNELS], U8, align_bytes=64)
        gain = keep.tile([P, CHANNELS], BF16)

        def transpose_x(a0, spread):
            x_words = x_sb[:].bitcast(F32).rearrange("r a (q u) -> r a u q", u=HALVES)
            x_grouped_words = x_grouped[:].bitcast(F32)
            x_apart = keep.tile([P, 2, HALVES, P], F32, name="x_apart%d" % a0)
            spread(out=x_apart[:], in_=x_words[:, a0 : a0 + 2])
            x_t = banks.tile([P, 2, HALVES, P], F32, tag="bank")
            for a in range(2):
                for u in range(HALVES):
                    nc.tensor.transpose(x_t[:, a, u, :], x_apart[:, a, u, :], ident[:])
            return lambda: nc.scalar.copy(
                out=x_grouped_words[:, a0 : a0 + 2],
                in_=x_t[:].rearrange("q a u r -> q a r u"),
            )

        def quantise_x(a0):
            rows = slice(a0 * P, (a0 + 2) * P)
            nc.vector.quantize_mx(
                out=x_codes[:, rows].bitcast(FP8X4),
                scales=x_scales[:, rows],
                in_=x_grouped[:, a0 : a0 + 2].rearrange("q a r k -> q (a r k)"),
            )

        def turn_gain():
            columns_ps = banks.tile([P, P], BF16, tag="bank")
            nc.tensor.transpose(columns_ps[:], gain_rows[:], ident_bf16[:])
            columns = keep.tile([P, 2], BF16)
            nc.scalar.copy(out=columns[:], in_=columns_ps[:, 0:2])
            return columns

        def spread_gain(columns):
            gain_ps = banks.tile([P, CHANNELS], BF16, tag="bank")
            for r in range(2):
                nc.tensor.transpose(
                    gain_ps[:, r * P : (r + 1) * P],
                    columns[:, r : r + 1].to_broadcast([P, P]),
                    ident_bf16[:],
                )
            nc.scalar.copy(out=gain[:], in_=gain_ps[:])

        w_sum = []
        for c in range(CHANNEL_TILES):
            bank = sums.tile([P, PACK, P], F32, tag="sum")
            w_sum.append(bank)

        def slots(l, c):
            rows = w_sb[:, l, c, :] if l < LAST else last_sb[:, c, l - LAST, :]
            return rows.rearrange("k (g q t) -> k g t q", q=2, t=PACK)

        def accumulate(c, term, ts, first=False, last=False, plain=()):
            for t in ts:
                nc.tensor.matmul(
                    out=w_sum[c][:, t, :],
                    lhsT=term[:, t, :],
                    rhs=ident[:],
                    start=first and t == 0,
                    stop=last and t == PACK - 1,
                    is_transpose=t not in plain,
                )

        def widened(l, c, ts):
            term = terms.tile([P, PACK, P], F32, tag="term")
            nc.scalar.copy(
                out=term[:, ts].rearrange("k t (g q) -> k g t q", q=2), in_=slots(l, c)[:, :, ts]
            )
            return term

        def pair_sum(l, c, ts):
            term = terms.tile([P, PACK, P], F32, tag="term")
            nc.vector.tensor_tensor(
                out=term[:, ts].rearrange("k t (g q) -> k g t q", q=2),
                in0=slots(l, c)[:, :, ts],
                in1=slots(l + 1, c)[:, :, ts],
                op=ADD,
            )
            return term

        every = slice(0, PACK)
        all_slots = range(PACK)
        def quantise_w(c):
            columns = slice(c * P, (c + 1) * P)
            nc.vector.quantize_mx(
                out=w_codes[:, columns].bitcast(FP8X4),
                scales=w_scales[:, columns],
                in_=w_grouped[:, c].rearrange("q p k -> q (p k)"),
            )

        for l in range(0, LAST, 2):
            for c in range(CHANNEL_TILES):
                plain = (3,) if (l, c) in ((0, 1), (4, 0), (6, 1)) else ()
                accumulate(c, pair_sum(l, c, every), all_slots, first=l == 0, plain=plain)
                if (l, c) == (0, 1):
                    gain_columns = turn_gain()
                if (l, c) == (2, 1):
                    spread_gain(gain_columns)
        copy_x0 = transpose_x(0, nc.scalar.copy)
        accumulate(0, pair_sum(LAST, 0, every), all_slots, last=True)
        for l in (LAST, LAST + 1):
            accumulate(1, widened(l, 1, slice(0, 1)), range(0, 1))
        accumulate(1, pair_sum(LAST, 1, slice(1, PACK)), range(1, PACK), last=True)
        copy_x0()
        copy_x2 = transpose_x(2, nc.vector.tensor_copy)
        nc.vector.tensor_copy(out=w_grouped[:, 0], in_=w_sum[0][:].rearrange("q t k -> q k t"))
        nc.scalar.copy(out=w_grouped[:, 1], in_=w_sum[1][:].rearrange("q t k -> q k t"))
        quantise_x(0)
        quantise_w(0)
        quantise_w(1)
        copy_x2()
        quantise_x(2)

        sum_sq = keep.tile([P, TOKEN_TILES], F32)
        inv_norm = keep.tile([P, TOKEN_TILES], F32)
        out_sb = keep.tile([P, TOKEN_TILES, CHANNELS], F32)
        y = []
        for a in range(TOKEN_TILES):
            rows = slice(a * P, (a + 1) * P)
            y_a = banks.tile([P, CHANNELS], F32, tag="bank")
            nc.tensor.matmul_mx(
                out=y_a[:],
                lhsT=x_codes[:, rows].bitcast(FP8X4),
                lhsT_scale=x_scales[:, rows],
                rhs=w_codes[:].bitcast(FP8X4),
                rhs_scale=w_scales[:],
                start=True,
                stop=True,
            )
            y.append(y_a)

        def square(a):
            squares = stage.tile([P, CHANNELS], F32)
            nc.scalar.activation(
                out=squares[:],
                in_=y[a][:],
                func=FUNC.Square,
                accum_out=sum_sq[:, a : a + 1],
            )

        def normalise(a):
            nc.scalar.activation(
                out=inv_norm[:, a : a + 1],
                in_=sum_sq[:, a : a + 1],
                func=FUNC.Abs_reciprocal_sqrt,
                scale=1.0 / H,
                bias=EPS * LAYERS**2,
            )
            nc.vector.scalar_tensor_tensor(
                out=out_sb[:, a, :].rearrange("r (p c) -> r p c", c=CHANNEL_TILES),
                in0=y[a][:].rearrange("r (c p) -> r p c", c=CHANNEL_TILES),
                scalar=inv_norm[:, a : a + 1],
                in1=gain[:].rearrange("r (p c) -> r p c", c=CHANNEL_TILES),
                op0=MULT,
                op1=MULT,
            )
            nc.sync.dma_start(out=out_dram[:, a, :], in_=out_sb[:, a, :])

        square(0)
        for a in range(TOKEN_TILES):
            if a + 1 < TOKEN_TILES:
                square(a + 1)
            normalise(a)
